import numpy as np
import ml_dtypes


def mxq(x, axis, fmt="e4m3"):
    dtype, down = {"e4m3": (ml_dtypes.float8_e4m3fn, 7), "e5m2": (ml_dtypes.float8_e5m2, 14)}[fmt]
    v = np.moveaxis(np.asarray(x, np.float32).astype(ml_dtypes.bfloat16).astype(np.float64), axis, -1)
    blocks = v.reshape(v.shape[:-1] + (-1, 32))
    amax = np.abs(blocks).max(-1, keepdims=True)
    byte = np.maximum(np.where(amax > 0, np.frexp(amax)[1] - 1 + 127, 0) - down, 1)
    scale = np.exp2(byte - 127.0)
    codes = (blocks / scale).astype(np.float32).astype(dtype).astype(np.float64)
    return np.moveaxis((codes * scale).reshape(v.shape), -1, axis)


WIDE = False


def mx_kscale(k):
    if not WIDE:
        return np.ones(k)
    levels = np.array([10, -10, 5, -5, 0])
    a = np.random.permutation(np.resize(levels, k // 512 * 4)).reshape(k // 512, 4)
    idx = np.arange(k)
    return np.exp2(a[idx // 512, idx % 128 // 32])


BF16 = ml_dtypes.bfloat16


def bf(x):
    return np.asarray(x, np.float32).astype(BF16)


def f64(x):
    return np.asarray(x).astype(np.float64)


S, D = 512, 2048
HALF = D // 2
BASE = 10000.0


def rope_interleaved(v):
    freqs = 1.0 / BASE ** (np.arange(HALF) / HALF)
    ang = np.arange(S)[:, None] * freqs[None, :]
    cos, sin = np.cos(ang), np.sin(ang)
    vp = v.reshape(S, HALF, 2)
    vr, vi = vp[..., 0], vp[..., 1]
    rot = np.stack([vr * cos - vi * sin, vr * sin + vi * cos], axis=-1)
    return rot.reshape(S, D)


def setup_inputs():
    s = mx_kscale(D)
    return {"x": bf(np.random.standard_normal((S, D)) * s),
            "w": bf(np.random.standard_normal((D, D)) / np.sqrt(D) / s[None, :])}


def reference(x, w):
    y = mxq(f64(x), 1, "e4m3") @ mxq(f64(w), 1, "e4m3").T
    return rope_interleaved(y)

@@ -1,0 +1,240 @@
+import math
+from contextlib import ExitStack
+
+import concourse.mybir as mybir
+from concourse.masks import make_identity
+
+F32 = mybir.dt.float32
+BF16 = mybir.dt.bfloat16
+I32 = mybir.dt.int32
+U32 = mybir.dt.uint32
+U8 = mybir.dt.uint8
+FP8X4 = mybir.dt.float8_e4m3fn_x4
+ALU = mybir.AluOpType
+ACT = mybir.ActivationFunctionType
+
+P = 128
+S, D = 512, 2048
+HALF = D // 2
+BASE = 10000.0
+FLOPS = 2 * S * D * D
+
+NT = S // P
+NG = D // 512
+NU = 8
+TWO_PI = 2.0 * math.pi
+THR = (416, 496, 544, 576)
+CHUNKS = (3, 2, 1, 0)
+X_EVAC = ("v", "s")
+TURNS_ON_ACT = True
+P3_ON_POOL = (True, True)
+HEAD = 0
+
+
+def tile_ropeattention_pa_kernel(tc, x, w, out):
+    nc = tc.nc
+    with ExitStack() as ctx:
+        const = ctx.enter_context(tc.tile_pool(name="const", bufs=1))
+        big = ctx.enter_context(tc.tile_pool(name="big", bufs=1))
+        grp = ctx.enter_context(tc.tile_pool(name="grp", bufs=5))
+        codes = ctx.enter_context(tc.tile_pool(name="codes", bufs=3))
+        work = ctx.enter_context(tc.tile_pool(name="work", bufs=3))
+        psum = ctx.enter_context(tc.psum_pool(name="psum", bufs=4))
+        ctx.enter_context(tc.manual_schedule())
+
+        x_sb = [big.tile([P, D], BF16, name="x_sb%d" % t) for t in range(NT)]
+        w_sb = [big.tile([P, 2 * D], BF16, name="w_sb%d" % k) for k in range(NU)]
+
+        def unit_rows(k):
+            return CHUNKS[k // 2] * 512 + (k % 2) * 256
+
+        def load_x(t):
+            nc.sync.dma_start(out=x_sb[t][:], in_=x[t * P:(t + 1) * P, :])
+
+        def load_w(k):
+            r0 = unit_rows(k)
+            nc.sync.dma_start(out=w_sb[k][:], in_=w[r0:r0 + 256, :].rearrange("(p e) k -> p (e k)", e=2))
+
+        load_x(0)
+        load_w(0)
+        for t in range(1, NT):
+            load_x(t)
+        for k in range(1, NU):
+            load_w(k)
+
+        freq = const.tile([P, HALF], F32, name="freq")
+        nc.vector.memset(freq[:, 0:1], 1.0)
+        size = 1
+        while size < HALF:
+            for m in range(1, 4):
+                nc.vector.tensor_scalar(
+                    out=freq[:, m * size:(m + 1) * size], in0=freq[:, 0:size],
+                    scalar1=BASE ** (-(m * size) / HALF), scalar2=None, op0=ALU.mult,
+                )
+            size *= 4
+
+        s_int = const.tile([P, NT], I32, name="s_int")
+        nc.gpsimd.iota(s_int[:], pattern=[[P, NT]], base=0, channel_multiplier=1)
+        ident = const.tile([P, P], F32, name="ident")
+        make_identity(nc, ident[:])
+        sc = const.tile([P, 16], F32, name="sc")
+        nc.vector.tensor_copy(out=sc[:, 0:4], in_=s_int[:])
+        nc.vector.tensor_scalar(out=sc[:, 4:8], in0=sc[:, 0:4], scalar1=-1.0, scalar2=None, op0=ALU.mult)
+        nc.vector.tensor_scalar(out=sc[:, 8:12], in0=sc[:, 0:4], scalar1=1.0 / TWO_PI, scalar2=None, op0=ALU.mult)
+        nc.vector.memset(sc[:, 12:13], 1.0)
+        nc.vector.tensor_scalar(out=sc[:, 13:14], in0=sc[:, 12:13], scalar1=0.5 * math.pi, scalar2=None, op0=ALU.mult)
+        half_pi = sc[:, 13:14]
+
+        frac = [const.tile([P, THR[t]], F32, name="frac%d" % t) for t in range(NT)]
+        afr = [const.tile([P, THR[t]], F32, name="afr%d" % t) for t in range(NT)]
+        tab = [const.tile([P, NT, 3, 256], F32, name="tab%d" % n) for n in range(4)]
+
+        def reduce_turns(t):
+            hi = THR[t]
+            if TURNS_ON_ACT:
+                turns = work.tile([P, 576], U32, name="turns", bufs=2)
+                nc.scalar.activation(out=turns[:, 0:hi], in_=freq[:, 0:hi], func=ACT.Copy, scale=sc[:, 8 + t:9 + t])
+                tv = turns[:, 0:hi].bitcast(I32)
+            else:
+                turns = work.tile([P, 576], I32, name="turns", bufs=2)
+                nc.vector.tensor_scalar(out=turns[:, 0:hi], in0=freq[:, 0:hi], scalar1=sc[:, 8 + t:9 + t],
+                                        scalar2=None, op0=ALU.mult)
+                tv = turns[:, 0:hi]
+            nc.vector.scalar_tensor_tensor(out=frac[t][:, 0:hi], in0=freq[:, 0:hi], scalar=sc[:, 8 + t:9 + t],
+                                           in1=tv, op0=ALU.mult, op1=ALU.subtract)
+
+        def sin_cos(t, n):
+            lo, hi = 256 * n, 256 * (n + 1)
+            mid = min(max(THR[t], lo), hi)
+            if mid > lo:
+                nc.scalar.activation(out=afr[t][:, lo:mid], in_=frac[t][:, lo:mid], func=ACT.Abs)
+                nc.scalar.activation(out=tab[n][:, t, 2, 0:mid - lo], in_=frac[t][:, lo:mid], func=ACT.Sin,
+                                     scale=TWO_PI)
+                nc.scalar.activation(out=tab[n][:, t, 1, 0:mid - lo], in_=afr[t][:, lo:mid], func=ACT.Sin,
+                                     scale=-TWO_PI, bias=half_pi)
+            if mid < hi:
+                nc.scalar.activation(out=tab[n][:, t, 2, mid - lo:256], in_=freq[:, mid:hi], func=ACT.Sin,
+                                     scale=sc[:, t:t + 1])
+                nc.scalar.activation(out=tab[n][:, t, 1, mid - lo:256], in_=freq[:, mid:hi], func=ACT.Sin,
+                                     scale=sc[:, 4 + t:5 + t], bias=half_pi)
+
+        def tables_half(c, tp):
+            if c >= len(CHUNKS):
+                return
+            n = CHUNKS[c]
+            for t in (2 * tp, 2 * tp + 1):
+                sin_cos(t, n)
+            nc.gpsimd.tensor_scalar(out=tab[n][:, 2 * tp:2 * tp + 2, 0, :], in0=tab[n][:, 2 * tp:2 * tp + 2, 2, :],
+                                    scalar1=-1.0, scalar2=0.0, op0=ALU.mult, op1=ALU.add)
+
+        x_codes = [big.tile([P, 512], U32, name="x_codes%d" % t, align_bytes=64) for t in range(NT)]
+        x_scale = [big.tile([P, 512], U8, name="x_scale%d" % t, align_bytes=64) for t in range(NT)]
+
+        def x_tile(t):
+            xw = x_sb[t][:].bitcast(F32)
+            g4 = grp.tile([P, 2048], BF16, name="g4", align_bytes=64)
+            g4w = g4[:].bitcast(F32)
+            for b in range(2):
+                bank = psum.tile([P, 512], F32, name="tp")
+                for gl in range(2):
+                    for u in range(2):
+                        c = 2 * (2 * b + gl) + u
+                        nc.tensor.transpose(bank[:, (2 * gl + u) * P:(2 * gl + u + 1) * P],
+                                            xw[:, c * P:(c + 1) * P], ident[:])
+                dst = g4w[:, b * 512:(b + 1) * 512].rearrange("p (g r u) -> p g r u", g=2, u=2)
+                src = bank[:].rearrange("p (g u r) -> p g r u", g=2, u=2)
+                if X_EVAC[b] == "v":
+                    nc.vector.tensor_copy(out=dst, in_=src)
+                else:
+                    nc.scalar.copy(out=dst, in_=src)
+            nc.vector.quantize_mx(out=x_codes[t][:].bitcast(FP8X4), scales=x_scale[t][:], in_=g4[:])
+
+        w_codes = {}
+        w_scale = {}
+
+        def w_unit(k):
+            ww = w_sb[k][:].bitcast(F32)
+            w_codes[k] = codes.tile([P, 1024], U32, name="w_codes", align_bytes=64)
+            w_scale[k] = codes.tile([P, 1024], U8, name="w_scale", align_bytes=64)
+            for h in range(2):
+                g4 = grp.tile([P, 2048], BF16, name="g4", align_bytes=64)
+                g4w = g4[:].bitcast(F32)
+                for gl in range(2):
+                    g = 2 * h + gl
+                    bank = psum.tile([P, 512], F32, name="tp")
+                    for u in range(2):
+                        for e in range(2):
+                            c0 = e * 1024 + (2 * g + u) * P
+                            nc.tensor.transpose(bank[:, (2 * u + e) * P:(2 * u + e + 1) * P],
+                                                ww[:, c0:c0 + P], ident[:])
+                    nc.scalar.copy(
+                        out=g4w[:, gl * 512:(gl + 1) * 512].rearrange("p (c u) -> p c u", u=2),
+                        in_=bank[:].rearrange("p (u c) -> p c u", u=2),
+                    )
+                nc.vector.quantize_mx(out=w_codes[k][:, h * 512:(h + 1) * 512].bitcast(FP8X4),
+                                      scales=w_scale[k][:, h * 512:(h + 1) * 512], in_=g4[:])
+
+        o_tiles = {}
+
+        def mx_unit(k):
+            n, q = CHUNKS[k // 2], k % 2
+            for tp in range(2):
+                y = psum.tile([P, 512], F32, name="y")
+                for tt in range(2):
+                    t = 2 * tp + tt
+                    for g in range(NG):
+                        nc.tensor.matmul_mx(
+                            out=y[:, tt * 256:(tt + 1) * 256],
+                            lhsT=x_codes[t][:, g * P:(g + 1) * P].bitcast(FP8X4),
+                            lhsT_scale=x_scale[t][:, g * P:(g + 1) * P],
+                            rhs=w_codes[k][:, g * 256:(g + 1) * 256].bitcast(FP8X4),
+                            rhs_scale=w_scale[k][:, g * 256:(g + 1) * 256],
+                            start=(g == 0), stop=(g == NG - 1),
+                        )
+                yv = y[:].rearrange("p (t e r) -> p t e r", t=2, e=2)
+                pa = work.tile([P, 2, 2, P], F32, name="pa")
+                pb = work.tile([P, 2, 2, P], F32, name="pb")
+                cols = slice(q * P, (q + 1) * P)
+                nc.vector.tensor_tensor(out=pa[:], in0=yv[:, :, 0:1, :].to_broadcast([P, 2, 2, P]),
+                                        in1=tab[n][:, 2 * tp:2 * tp + 2, 1:3, cols], op=ALU.mult)
+                nc.vector.tensor_tensor(out=pb[:], in0=yv[:, :, 1:2, :].to_broadcast([P, 2, 2, P]),
+                                        in1=tab[n][:, 2 * tp:2 * tp + 2, 0:2, cols], op=ALU.mult)
+                if q == 0:
+                    o_tiles[tp] = work.tile([P, 2, 512], F32, name="o%d" % tp, bufs=2)
+                o = o_tiles[tp]
+                eng = nc.gpsimd if P3_ON_POOL[tp] else nc.vector
+                eng.tensor_tensor(
+                    out=o[:, :, q * 256:(q + 1) * 256].rearrange("p t (r e) -> p t r e", e=2),
+                    in0=pa[:].rearrange("p t e r -> p t r e"),
+                    in1=pb[:].rearrange("p t e r -> p t r e"),
+                    op=ALU.add,
+                )
+                if q == 1:
+                    nc.sync.dma_start(
+                        out=out[2 * tp * P:(2 * tp + 2) * P, n * 512:(n + 1) * 512].rearrange("(t p) c -> p t c", p=P),
+                        in_=o[:],
+                    )
+
+        for t in range(NT):
+            reduce_turns(t)
+        if HEAD == 0:
+            x_tile(0)
+            w_unit(0)
+            for t in range(1, NT):
+                x_tile(t)
+            tables_half(0, 0)
+            tables_half(0, 1)
+        elif HEAD == 1:
+            tables_half(0, 0)
+            x_tile(0)
+            w_unit(0)
+            tables_half(0, 1)
+            for t in range(1, NT):
+                x_tile(t)
+        mx_unit(0)
+        for k in range(1, NU + 1):
+            if k < NU:
+                w_unit(k)
+                tables_half((k + 1) // 2, (k + 1) % 2)
+            if k > 1:
+                mx_unit(k - 1)

@@ -27,7 +27,7 @@ THR = (416, 496, 544, 576)
 CHUNKS = (3, 2, 1, 0)
 X_EVAC = ("v", "s")
 TURNS_ON_ACT = True
-P3_ON_POOL = (True, True)
+P3_ON_POOL = (True, False)
 HEAD = 0
 
 
@@ -87,7 +87,7 @@ def tile_ropeattention_pa_kernel(tc, x, w, out):
 
         frac = [const.tile([P, THR[t]], F32, name="frac%d" % t) for t in range(NT)]
         afr = [const.tile([P, THR[t]], F32, name="afr%d" % t) for t in range(NT)]
-        tab = [const.tile([P, NT, 3, 256], F32, name="tab%d" % n) for n in range(4)]
+        tab = [const.tile([P, NT, 2, 256], F32, name="tab%d" % n) for n in range(4)]
 
         def reduce_turns(t):
             hi = THR[t]
@@ -108,14 +108,14 @@ def tile_ropeattention_pa_kernel(tc, x, w, out):
             mid = min(max(THR[t], lo), hi)
             if mid > lo:
                 nc.scalar.activation(out=afr[t][:, lo:mid], in_=frac[t][:, lo:mid], func=ACT.Abs)
-                nc.scalar.activation(out=tab[n][:, t, 2, 0:mid - lo], in_=frac[t][:, lo:mid], func=ACT.Sin,
+                nc.scalar.activation(out=tab[n][:, t, 1, 0:mid - lo], in_=frac[t][:, lo:mid], func=ACT.Sin,
                                      scale=TWO_PI)
-                nc.scalar.activation(out=tab[n][:, t, 1, 0:mid - lo], in_=afr[t][:, lo:mid], func=ACT.Sin,
+                nc.scalar.activation(out=tab[n][:, t, 0, 0:mid - lo], in_=afr[t][:, lo:mid], func=ACT.Sin,
                                      scale=-TWO_PI, bias=half_pi)
             if mid < hi:
-                nc.scalar.activation(out=tab[n][:, t, 2, mid - lo:256], in_=freq[:, mid:hi], func=ACT.Sin,
-                                     scale=sc[:, t:t + 1])
                 nc.scalar.activation(out=tab[n][:, t, 1, mid - lo:256], in_=freq[:, mid:hi], func=ACT.Sin,
+                                     scale=sc[:, t:t + 1])
+                nc.scalar.activation(out=tab[n][:, t, 0, mid - lo:256], in_=freq[:, mid:hi], func=ACT.Sin,
                                      scale=sc[:, 4 + t:5 + t], bias=half_pi)
 
         def tables_half(c, tp):
@@ -124,8 +124,6 @@ def tile_ropeattention_pa_kernel(tc, x, w, out):
             n = CHUNKS[c]
             for t in (2 * tp, 2 * tp + 1):
                 sin_cos(t, n)
-            nc.gpsimd.tensor_scalar(out=tab[n][:, 2 * tp:2 * tp + 2, 0, :], in0=tab[n][:, 2 * tp:2 * tp + 2, 2, :],
-                                    scalar1=-1.0, scalar2=0.0, op0=ALU.mult, op1=ALU.add)
 
         x_codes = [big.tile([P, 512], U32, name="x_codes%d" % t, align_bytes=64) for t in range(NT)]
         x_scale = [big.tile([P, 512], U8, name="x_scale%d" % t, align_bytes=64) for t in range(NT)]
@@ -196,9 +194,11 @@ def tile_ropeattention_pa_kernel(tc, x, w, out):
                 pb = work.tile([P, 2, 2, P], F32, name="pb")
                 cols = slice(q * P, (q + 1) * P)
                 nc.vector.tensor_tensor(out=pa[:], in0=yv[:, :, 0:1, :].to_broadcast([P, 2, 2, P]),
-                                        in1=tab[n][:, 2 * tp:2 * tp + 2, 1:3, cols], op=ALU.mult)
-                nc.vector.tensor_tensor(out=pb[:], in0=yv[:, :, 1:2, :].to_broadcast([P, 2, 2, P]),
-                                        in1=tab[n][:, 2 * tp:2 * tp + 2, 0:2, cols], op=ALU.mult)
+                                        in1=tab[n][:, 2 * tp:2 * tp + 2, :, cols], op=ALU.mult)
+                nc.vector.scalar_tensor_tensor(out=pb[:, :, 0, :], in0=yv[:, :, 1, :], scalar=-1.0,
+                                               in1=tab[n][:, 2 * tp:2 * tp + 2, 1, cols], op0=ALU.mult, op1=ALU.mult)
+                nc.vector.tensor_tensor(out=pb[:, :, 1, :], in0=yv[:, :, 1, :],
+                                        in1=tab[n][:, 2 * tp:2 * tp + 2, 0, cols], op=ALU.mult)
                 if q == 0:
                     o_tiles[tp] = work.tile([P, 2, 512], F32, name="o%d" % tp, bufs=2)
                 o = o_tiles[tp]

@@ -27,8 +27,9 @@ THR = (416, 496, 544, 576)
 CHUNKS = (3, 2, 1, 0)
 X_EVAC = ("v", "s")
 TURNS_ON_ACT = True
-P3_ON_POOL = (True, False)
 HEAD = 0
+W_EVAC_V = 0
+P3_MODE = "half"
 
 
 def tile_ropeattention_pa_kernel(tc, x, w, out):
@@ -45,15 +46,13 @@ def tile_ropeattention_pa_kernel(tc, x, w, out):
         x_sb = [big.tile([P, D], BF16, name="x_sb%d" % t) for t in range(NT)]
         w_sb = [big.tile([P, 2 * D], BF16, name="w_sb%d" % k) for k in range(NU)]
 
-        def unit_rows(k):
-            return CHUNKS[k // 2] * 512 + (k % 2) * 256
-
         def load_x(t):
             nc.sync.dma_start(out=x_sb[t][:], in_=x[t * P:(t + 1) * P, :])
 
         def load_w(k):
-            r0 = unit_rows(k)
-            nc.sync.dma_start(out=w_sb[k][:], in_=w[r0:r0 + 256, :].rearrange("(p e) k -> p (e k)", e=2))
+            n, e = CHUNKS[k // 2], k % 2
+            rows = w[n * 512:(n + 1) * 512, :].rearrange("(a p e) k -> e p a k", a=2, e=2)
+            nc.sync.dma_start(out=w_sb[k][:].rearrange("p (a k) -> p a k", a=2), in_=rows[e])
 
         load_x(0)
         load_w(0)
@@ -61,6 +60,21 @@ def tile_ropeattention_pa_kernel(tc, x, w, out):
             load_x(t)
         for k in range(1, NU):
             load_w(k)
+
+        warm = const.tile([P, 2], F32, name="warm")
+        nc.vector.memset(warm[:, 0:1], 0.0)
+        nc.scalar.activation(out=warm[:, 1:2], in_=warm[:, 0:1], func=ACT.Sin)
+        ident = const.tile([P, P], F32, name="ident")
+        make_identity(nc, ident[:])
+        s_int = const.tile([P, NT], I32, name="s_int")
+        nc.gpsimd.iota(s_int[:], pattern=[[P, NT]], base=0, channel_multiplier=1)
+        sc = const.tile([P, 16], F32, name="sc")
+        nc.vector.tensor_copy(out=sc[:, 0:4], in_=s_int[:])
+        nc.vector.tensor_scalar(out=sc[:, 4:8], in0=sc[:, 0:4], scalar1=-1.0, scalar2=None, op0=ALU.mult)
+        nc.vector.tensor_scalar(out=sc[:, 8:12], in0=sc[:, 0:4], scalar1=1.0 / TWO_PI, scalar2=None, op0=ALU.mult)
+        nc.vector.memset(sc[:, 12:13], 1.0)
+        nc.vector.tensor_scalar(out=sc[:, 13:14], in0=sc[:, 12:13], scalar1=0.5 * math.pi, scalar2=None, op0=ALU.mult)
+        half_pi = sc[:, 13:14]
 
         freq = const.tile([P, HALF], F32, name="freq")
         nc.vector.memset(freq[:, 0:1], 1.0)
@@ -73,21 +87,9 @@ def tile_ropeattention_pa_kernel(tc, x, w, out):
                 )
             size *= 4
 
-        s_int = const.tile([P, NT], I32, name="s_int")
-        nc.gpsimd.iota(s_int[:], pattern=[[P, NT]], base=0, channel_multiplier=1)
-        ident = const.tile([P, P], F32, name="ident")
-        make_identity(nc, ident[:])
-        sc = const.tile([P, 16], F32, name="sc")
-        nc.vector.tensor_copy(out=sc[:, 0:4], in_=s_int[:])
-        nc.vector.tensor_scalar(out=sc[:, 4:8], in0=sc[:, 0:4], scalar1=-1.0, scalar2=None, op0=ALU.mult)
-        nc.vector.tensor_scalar(out=sc[:, 8:12], in0=sc[:, 0:4], scalar1=1.0 / TWO_PI, scalar2=None, op0=ALU.mult)
-        nc.vector.memset(sc[:, 12:13], 1.0)
-        nc.vector.tensor_scalar(out=sc[:, 13:14], in0=sc[:, 12:13], scalar1=0.5 * math.pi, scalar2=None, op0=ALU.mult)
-        half_pi = sc[:, 13:14]
-
         frac = [const.tile([P, THR[t]], F32, name="frac%d" % t) for t in range(NT)]
         afr = [const.tile([P, THR[t]], F32, name="afr%d" % t) for t in range(NT)]
-        tab = [const.tile([P, NT, 2, 256], F32, name="tab%d" % n) for n in range(4)]
+        tab = [const.tile([P, NT, 3, 256], F32, name="tab%d" % n) for n in range(4)]
 
         def reduce_turns(t):
             hi = THR[t]
@@ -108,14 +110,14 @@ def tile_ropeattention_pa_kernel(tc, x, w, out):
             mid = min(max(THR[t], lo), hi)
             if mid > lo:
                 nc.scalar.activation(out=afr[t][:, lo:mid], in_=frac[t][:, lo:mid], func=ACT.Abs)
-                nc.scalar.activation(out=tab[n][:, t, 1, 0:mid - lo], in_=frac[t][:, lo:mid], func=ACT.Sin,
+                nc.scalar.activation(out=tab[n][:, t, 2, 0:mid - lo], in_=frac[t][:, lo:mid], func=ACT.Sin,
                                      scale=TWO_PI)
-                nc.scalar.activation(out=tab[n][:, t, 0, 0:mid - lo], in_=afr[t][:, lo:mid], func=ACT.Sin,
+                nc.scalar.activation(out=tab[n][:, t, 1, 0:mid - lo], in_=afr[t][:, lo:mid], func=ACT.Sin,
                                      scale=-TWO_PI, bias=half_pi)
             if mid < hi:
-                nc.scalar.activation(out=tab[n][:, t, 1, mid - lo:256], in_=freq[:, mid:hi], func=ACT.Sin,
+                nc.scalar.activation(out=tab[n][:, t, 2, mid - lo:256], in_=freq[:, mid:hi], func=ACT.Sin,
                                      scale=sc[:, t:t + 1])
-                nc.scalar.activation(out=tab[n][:, t, 0, mid - lo:256], in_=freq[:, mid:hi], func=ACT.Sin,
+                nc.scalar.activation(out=tab[n][:, t, 1, mid - lo:256], in_=freq[:, mid:hi], func=ACT.Sin,
                                      scale=sc[:, 4 + t:5 + t], bias=half_pi)
 
         def tables_half(c, tp):
@@ -124,6 +126,8 @@ def tile_ropeattention_pa_kernel(tc, x, w, out):
             n = CHUNKS[c]
             for t in (2 * tp, 2 * tp + 1):
                 sin_cos(t, n)
+            nc.gpsimd.tensor_scalar(out=tab[n][:, 2 * tp:2 * tp + 2, 0, :], in0=tab[n][:, 2 * tp:2 * tp + 2, 2, :],
+                                    scalar1=-1.0, scalar2=0.0, op0=ALU.mult, op1=ALU.add)
 
         x_codes = [big.tile([P, 512], U32, name="x_codes%d" % t, align_bytes=64) for t in range(NT)]
         x_scale = [big.tile([P, 512], U8, name="x_scale%d" % t, align_bytes=64) for t in range(NT)]
@@ -165,17 +169,19 @@ def tile_ropeattention_pa_kernel(tc, x, w, out):
                             c0 = e * 1024 + (2 * g + u) * P
                             nc.tensor.transpose(bank[:, (2 * u + e) * P:(2 * u + e + 1) * P],
                                                 ww[:, c0:c0 + P], ident[:])
-                    nc.scalar.copy(
-                        out=g4w[:, gl * 512:(gl + 1) * 512].rearrange("p (c u) -> p c u", u=2),
-                        in_=bank[:].rearrange("p (u c) -> p c u", u=2),
-                    )
+                    dst = g4w[:, gl * 512:(gl + 1) * 512].rearrange("p (c u) -> p c u", u=2)
+                    src = bank[:].rearrange("p (u c) -> p c u", u=2)
+                    if k < W_EVAC_V and gl == 1:
+                        nc.vector.tensor_copy(out=dst, in_=src)
+                    else:
+                        nc.scalar.copy(out=dst, in_=src)
                 nc.vector.quantize_mx(out=w_codes[k][:, h * 512:(h + 1) * 512].bitcast(FP8X4),
                                       scales=w_scale[k][:, h * 512:(h + 1) * 512], in_=g4[:])
 
-        o_tiles = {}
+        first_products = {}
 
         def mx_unit(k):
-            n, q = CHUNKS[k // 2], k % 2
+            n, e = CHUNKS[k // 2], k % 2
             for tp in range(2):
                 y = psum.tile([P, 512], F32, name="y")
                 for tt in range(2):
@@ -189,31 +195,24 @@ def tile_ropeattention_pa_kernel(tc, x, w, out):
                             rhs_scale=w_scale[k][:, g * 256:(g + 1) * 256],
                             start=(g == 0), stop=(g == NG - 1),
                         )
-                yv = y[:].rearrange("p (t e r) -> p t e r", t=2, e=2)
-                pa = work.tile([P, 2, 2, P], F32, name="pa")
-                pb = work.tile([P, 2, 2, P], F32, name="pb")
-                cols = slice(q * P, (q + 1) * P)
-                nc.vector.tensor_tensor(out=pa[:], in0=yv[:, :, 0:1, :].to_broadcast([P, 2, 2, P]),
-                                        in1=tab[n][:, 2 * tp:2 * tp + 2, :, cols], op=ALU.mult)
-                nc.vector.scalar_tensor_tensor(out=pb[:, :, 0, :], in0=yv[:, :, 1, :], scalar=-1.0,
-                                               in1=tab[n][:, 2 * tp:2 * tp + 2, 1, cols], op0=ALU.mult, op1=ALU.mult)
-                nc.vector.tensor_tensor(out=pb[:, :, 1, :], in0=yv[:, :, 1, :],
-                                        in1=tab[n][:, 2 * tp:2 * tp + 2, 0, cols], op=ALU.mult)
-                if q == 0:
-                    o_tiles[tp] = work.tile([P, 2, 512], F32, name="o%d" % tp, bufs=2)
-                o = o_tiles[tp]
-                eng = nc.gpsimd if P3_ON_POOL[tp] else nc.vector
-                eng.tensor_tensor(
-                    out=o[:, :, q * 256:(q + 1) * 256].rearrange("p t (r e) -> p t r e", e=2),
-                    in0=pa[:].rearrange("p t e r -> p t r e"),
-                    in1=pb[:].rearrange("p t e r -> p t r e"),
-                    op=ALU.add,
+                prod = work.tile([P, 2, 256, 2], F32, name="pa" if e == 0 else "pb", bufs=4 if e == 0 else 3)
+                nc.vector.tensor_tensor(
+                    out=prod[:],
+                    in0=y[:].rearrange("p (t r) -> p t r", t=2).unsqueeze(3).to_broadcast([P, 2, 256, 2]),
+                    in1=tab[n][:, 2 * tp:2 * tp + 2, 1 - e:3 - e, :].rearrange("p t c r -> p t r c"),
+                    op=ALU.mult,
                 )
-                if q == 1:
-                    nc.sync.dma_start(
-                        out=out[2 * tp * P:(2 * tp + 2) * P, n * 512:(n + 1) * 512].rearrange("(t p) c -> p t c", p=P),
-                        in_=o[:],
-                    )
+                if e == 0:
+                    first_products[tp] = prod
+                else:
+                    res = first_products[tp]
+                    on_vector = (k == NU - 1 and tp == 1) or (P3_MODE == "half" and tp == 1) or P3_MODE == "dve"
+                    eng = nc.vector if on_vector else nc.gpsimd
+                    for tt in range(2):
+                        t = 2 * tp + tt
+                        eng.tensor_tensor(out=res[:, tt], in0=res[:, tt], in1=prod[:, tt], op=ALU.add)
+                        nc.sync.dma_start(out=out[t * P:(t + 1) * P, n * 512:(n + 1) * 512],
+                                          in_=res[:, tt].rearrange("p r c -> p (r c)"))
 
         for t in range(NT):
             reduce_turns(t)

@@ -25,11 +25,11 @@ NU = 8
 TWO_PI = 2.0 * math.pi
 THR = (416, 496, 544, 576)
 CHUNKS = (3, 2, 1, 0)
-X_EVAC = ("v", "s")
+X_EVAC = ("s", "s")
 TURNS_ON_ACT = True
 HEAD = 0
-W_EVAC_V = 0
-P3_MODE = "half"
+W_EVAC_V = 2
+P3_MODE = "pool"
 
 
 def tile_ropeattention_pa_kernel(tc, x, w, out):

@@ -154,11 +154,12 @@ def tile_ropeattention_pa_kernel(tc, x, w, out):
         w_codes = {}
         w_scale = {}
 
-        def w_unit(k):
+        def w_unit(k, halves=(0, 1)):
             ww = w_sb[k][:].bitcast(F32)
-            w_codes[k] = codes.tile([P, 1024], U32, name="w_codes", align_bytes=64)
-            w_scale[k] = codes.tile([P, 1024], U8, name="w_scale", align_bytes=64)
-            for h in range(2):
+            if 0 in halves:
+                w_codes[k] = codes.tile([P, 1024], U32, name="w_codes", align_bytes=64)
+                w_scale[k] = codes.tile([P, 1024], U8, name="w_scale", align_bytes=64)
+            for h in halves:
                 g4 = grp.tile([P, 2048], BF16, name="g4", align_bytes=64)
                 g4w = g4[:].bitcast(F32)
                 for gl in range(2):
@@ -180,9 +181,9 @@ def tile_ropeattention_pa_kernel(tc, x, w, out):
 
         first_products = {}
 
-        def mx_unit(k):
+        def mx_unit(k, tps=(0, 1)):
             n, e = CHUNKS[k // 2], k % 2
-            for tp in range(2):
+            for tp in tps:
                 y = psum.tile([P, 512], F32, name="y")
                 for tt in range(2):
                     t = 2 * tp + tt
@@ -231,9 +232,12 @@ def tile_ropeattention_pa_kernel(tc, x, w, out):
             for t in range(1, NT):
                 x_tile(t)
         mx_unit(0)
-        for k in range(1, NU + 1):
-            if k < NU:
-                w_unit(k)
-                tables_half((k + 1) // 2, (k + 1) % 2)
-            if k > 1:
-                mx_unit(k - 1)
+        w_unit(1)
+        tables_half(1, 0)
+        for k in range(2, NU + 1):
+            for h in range(2):
+                if k < NU:
+                    w_unit(k, (h,))
+                    if h == 1:
+                        tables_half((k + 1) // 2, (k + 1) % 2)
+                mx_unit(k - 1, (h,))

@@ -41,7 +41,6 @@ def tile_ropeattention_pa_kernel(tc, x, w, out):
         codes = ctx.enter_context(tc.tile_pool(name="codes", bufs=3))
         work = ctx.enter_context(tc.tile_pool(name="work", bufs=3))
         psum = ctx.enter_context(tc.psum_pool(name="psum", bufs=4))
-        ctx.enter_context(tc.manual_schedule())
 
         x_sb = [big.tile([P, D], BF16, name="x_sb%d" % t) for t in range(NT)]
         w_sb = [big.tile([P, 2 * D], BF16, name="w_sb%d" % k) for k in range(NU)]
@@ -154,12 +153,11 @@ def tile_ropeattention_pa_kernel(tc, x, w, out):
         w_codes = {}
         w_scale = {}
 
-        def w_unit(k, halves=(0, 1)):
+        def w_unit(k):
             ww = w_sb[k][:].bitcast(F32)
-            if 0 in halves:
-                w_codes[k] = codes.tile([P, 1024], U32, name="w_codes", align_bytes=64)
-                w_scale[k] = codes.tile([P, 1024], U8, name="w_scale", align_bytes=64)
-            for h in halves:
+            w_codes[k] = codes.tile([P, 1024], U32, name="w_codes", align_bytes=64)
+            w_scale[k] = codes.tile([P, 1024], U8, name="w_scale", align_bytes=64)
+            for h in range(2):
                 g4 = grp.tile([P, 2048], BF16, name="g4", align_bytes=64)
                 g4w = g4[:].bitcast(F32)
                 for gl in range(2):
@@ -181,9 +179,9 @@ def tile_ropeattention_pa_kernel(tc, x, w, out):
 
         first_products = {}
 
-        def mx_unit(k, tps=(0, 1)):
+        def mx_unit(k):
             n, e = CHUNKS[k // 2], k % 2
-            for tp in tps:
+            for tp in range(2):
                 y = psum.tile([P, 512], F32, name="y")
                 for tt in range(2):
                     t = 2 * tp + tt
@@ -232,12 +230,9 @@ def tile_ropeattention_pa_kernel(tc, x, w, out):
             for t in range(1, NT):
                 x_tile(t)
         mx_unit(0)
-        w_unit(1)
-        tables_half(1, 0)
-        for k in range(2, NU + 1):
-            for h in range(2):
-                if k < NU:
-                    w_unit(k, (h,))
-                    if h == 1:
-                        tables_half((k + 1) // 2, (k + 1) % 2)
-                mx_unit(k - 1, (h,))
+        for k in range(1, NU + 1):
+            if k < NU:
+                w_unit(k)
+                tables_half((k + 1) // 2, (k + 1) % 2)
+            if k > 1:
+                mx_unit(k - 1)

@@ -23,13 +23,12 @@ NT = S // P
 NG = D // 512
 NU = 8
 TWO_PI = 2.0 * math.pi
-THR = (416, 496, 544, 576)
+THR = (496, 576)
 CHUNKS = (3, 2, 1, 0)
 X_EVAC = ("s", "s")
-TURNS_ON_ACT = True
 HEAD = 0
 W_EVAC_V = 2
-P3_MODE = "pool"
+LAST_ON_VECTOR = 2
 
 
 def tile_ropeattention_pa_kernel(tc, x, w, out):
@@ -86,46 +85,37 @@ def tile_ropeattention_pa_kernel(tc, x, w, out):
                 )
             size *= 4
 
-        frac = [const.tile([P, THR[t]], F32, name="frac%d" % t) for t in range(NT)]
-        afr = [const.tile([P, THR[t]], F32, name="afr%d" % t) for t in range(NT)]
+        frac = [const.tile([P, 2, THR[tp]], F32, name="frac%d" % tp) for tp in range(2)]
+        afr = [const.tile([P, 2, THR[tp]], F32, name="afr%d" % tp) for tp in range(2)]
         tab = [const.tile([P, NT, 3, 256], F32, name="tab%d" % n) for n in range(4)]
 
         def reduce_turns(t):
-            hi = THR[t]
-            if TURNS_ON_ACT:
-                turns = work.tile([P, 576], U32, name="turns", bufs=2)
-                nc.scalar.activation(out=turns[:, 0:hi], in_=freq[:, 0:hi], func=ACT.Copy, scale=sc[:, 8 + t:9 + t])
-                tv = turns[:, 0:hi].bitcast(I32)
-            else:
-                turns = work.tile([P, 576], I32, name="turns", bufs=2)
-                nc.vector.tensor_scalar(out=turns[:, 0:hi], in0=freq[:, 0:hi], scalar1=sc[:, 8 + t:9 + t],
-                                        scalar2=None, op0=ALU.mult)
-                tv = turns[:, 0:hi]
-            nc.vector.scalar_tensor_tensor(out=frac[t][:, 0:hi], in0=freq[:, 0:hi], scalar=sc[:, 8 + t:9 + t],
-                                           in1=tv, op0=ALU.mult, op1=ALU.subtract)
-
-        def sin_cos(t, n):
-            lo, hi = 256 * n, 256 * (n + 1)
-            mid = min(max(THR[t], lo), hi)
-            if mid > lo:
-                nc.scalar.activation(out=afr[t][:, lo:mid], in_=frac[t][:, lo:mid], func=ACT.Abs)
-                nc.scalar.activation(out=tab[n][:, t, 2, 0:mid - lo], in_=frac[t][:, lo:mid], func=ACT.Sin,
-                                     scale=TWO_PI)
-                nc.scalar.activation(out=tab[n][:, t, 1, 0:mid - lo], in_=afr[t][:, lo:mid], func=ACT.Sin,
-                                     scale=-TWO_PI, bias=half_pi)
-            if mid < hi:
-                nc.scalar.activation(out=tab[n][:, t, 2, mid - lo:256], in_=freq[:, mid:hi], func=ACT.Sin,
-                                     scale=sc[:, t:t + 1])
-                nc.scalar.activation(out=tab[n][:, t, 1, mid - lo:256], in_=freq[:, mid:hi], func=ACT.Sin,
-                                     scale=sc[:, 4 + t:5 + t], bias=half_pi)
+            hi = THR[t // 2]
+            turns = work.tile([P, 576], U32, name="turns", bufs=2)
+            nc.scalar.activation(out=turns[:, 0:hi], in_=freq[:, 0:hi], func=ACT.Copy, scale=sc[:, 8 + t:9 + t])
+            nc.vector.scalar_tensor_tensor(out=frac[t // 2][:, t % 2, :], in0=freq[:, 0:hi], scalar=sc[:, 8 + t:9 + t],
+                                           in1=turns[:, 0:hi].bitcast(I32), op0=ALU.mult, op1=ALU.subtract)
 
         def tables_half(c, tp):
             if c >= len(CHUNKS):
                 return
             n = CHUNKS[c]
-            for t in (2 * tp, 2 * tp + 1):
-                sin_cos(t, n)
-            nc.gpsimd.tensor_scalar(out=tab[n][:, 2 * tp:2 * tp + 2, 0, :], in0=tab[n][:, 2 * tp:2 * tp + 2, 2, :],
+            lo, hi = 256 * n, 256 * (n + 1)
+            mid = min(max(THR[tp], lo), hi)
+            both = slice(2 * tp, 2 * tp + 2)
+            if mid > lo:
+                nc.scalar.activation(out=afr[tp][:, :, lo:mid], in_=frac[tp][:, :, lo:mid], func=ACT.Abs)
+                nc.scalar.activation(out=tab[n][:, both, 2, 0:mid - lo], in_=frac[tp][:, :, lo:mid], func=ACT.Sin,
+                                     scale=TWO_PI)
+                nc.scalar.activation(out=tab[n][:, both, 1, 0:mid - lo], in_=afr[tp][:, :, lo:mid], func=ACT.Sin,
+                                     scale=-TWO_PI, bias=half_pi)
+            if mid < hi:
+                for t in (2 * tp, 2 * tp + 1):
+                    nc.scalar.activation(out=tab[n][:, t, 2, mid - lo:256], in_=freq[:, mid:hi], func=ACT.Sin,
+                                         scale=sc[:, t:t + 1])
+                    nc.scalar.activation(out=tab[n][:, t, 1, mid - lo:256], in_=freq[:, mid:hi], func=ACT.Sin,
+                                         scale=sc[:, 4 + t:5 + t], bias=half_pi)
+            nc.gpsimd.tensor_scalar(out=tab[n][:, both, 0, :], in0=tab[n][:, both, 2, :],
                                     scalar1=-1.0, scalar2=0.0, op0=ALU.mult, op1=ALU.add)
 
         x_codes = [big.tile([P, 512], U32, name="x_codes%d" % t, align_bytes=64) for t in range(NT)]
@@ -181,13 +171,15 @@ def tile_ropeattention_pa_kernel(tc, x, w, out):
 
         def mx_unit(k):
             n, e = CHUNKS[k // 2], k % 2
-            for tp in range(2):
-                y = psum.tile([P, 512], F32, name="y")
-                for tt in range(2):
-                    t = 2 * tp + tt
+            last = k == NU - 1
+            groups = [(t,) for t in range(NT)] if last else [(0, 1), (2, 3)]
+            for tiles in groups:
+                nt = len(tiles)
+                y = psum.tile([P, 512], F32, name="tp" if last else "y")
+                for j, t in enumerate(tiles):
                     for g in range(NG):
                         nc.tensor.matmul_mx(
-                            out=y[:, tt * 256:(tt + 1) * 256],
+                            out=y[:, j * 256:(j + 1) * 256],
                             lhsT=x_codes[t][:, g * P:(g + 1) * P].bitcast(FP8X4),
                             lhsT_scale=x_scale[t][:, g * P:(g + 1) * P],
                             rhs=w_codes[k][:, g * 256:(g + 1) * 256].bitcast(FP8X4),
@@ -196,22 +188,20 @@ def tile_ropeattention_pa_kernel(tc, x, w, out):
                         )
                 prod = work.tile([P, 2, 256, 2], F32, name="pa" if e == 0 else "pb", bufs=4 if e == 0 else 3)
                 nc.vector.tensor_tensor(
-                    out=prod[:],
-                    in0=y[:].rearrange("p (t r) -> p t r", t=2).unsqueeze(3).to_broadcast([P, 2, 256, 2]),
-                    in1=tab[n][:, 2 * tp:2 * tp + 2, 1 - e:3 - e, :].rearrange("p t c r -> p t r c"),
+                    out=prod[:, 0:nt],
+                    in0=y[:, 0:nt * 256].rearrange("p (t r) -> p t r", t=nt).unsqueeze(3).to_broadcast([P, nt, 256, 2]),
+                    in1=tab[n][:, tiles[0]:tiles[0] + nt, 1 - e:3 - e, :].rearrange("p t c r -> p t r c"),
                     op=ALU.mult,
                 )
                 if e == 0:
-                    first_products[tp] = prod
+                    first_products[tiles[0] // 2] = prod
                 else:
-                    res = first_products[tp]
-                    on_vector = (k == NU - 1 and tp == 1) or (P3_MODE == "half" and tp == 1) or P3_MODE == "dve"
-                    eng = nc.vector if on_vector else nc.gpsimd
-                    for tt in range(2):
-                        t = 2 * tp + tt
-                        eng.tensor_tensor(out=res[:, tt], in0=res[:, tt], in1=prod[:, tt], op=ALU.add)
+                    eng = nc.vector if (last and tiles[0] >= LAST_ON_VECTOR) else nc.gpsimd
+                    for j, t in enumerate(tiles):
+                        res = first_products[t // 2][:, t % 2]
+                        eng.tensor_tensor(out=res, in0=res, in1=prod[:, j], op=ALU.add)
                         nc.sync.dma_start(out=out[t * P:(t + 1) * P, n * 512:(n + 1) * 512],
-                                          in_=res[:, tt].rearrange("p r c -> p (r c)"))
+                                          in_=res.rearrange("p r c -> p (r c)"))
 
         for t in range(NT):
             reduce_turns(t)

@@ -14,215 +14,226 @@ ALU = mybir.AluOpType
 ACT = mybir.ActivationFunctionType
 
 P = 128
-S, D = 512, 2048
-HALF = D // 2
+TOKENS, WIDTH = 512, 2048
+PAIRS = WIDTH // 2
 BASE = 10000.0
-FLOPS = 2 * S * D * D
+FLOPS = 2 * TOKENS * WIDTH * WIDTH
 
-NT = S // P
-NG = D // 512
-NU = 8
+BANK = 512
+TOKEN_TILES = TOKENS // P
+PASSES = WIDTH // (4 * P)
+CHUNK_PAIRS = 256
+CHUNK_ORDER = (3, 2, 1, 0)
+UNITS = 2 * len(CHUNK_ORDER)
+SHARED_UNITS = 2
 TWO_PI = 2.0 * math.pi
-THR = (496, 576)
-CHUNKS = (3, 2, 1, 0)
-X_EVAC = ("s", "s")
-HEAD = 0
-W_EVAC_V = 2
-LAST_ON_VECTOR = 2
+
+
+def first_small_pair(row):
+    pair = 0
+    while row * BASE ** (-pair / PAIRS) > math.pi:
+        pair += 16
+    return pair
 
 
 def tile_ropeattention_pa_kernel(tc, x, w, out):
     nc = tc.nc
     with ExitStack() as ctx:
         const = ctx.enter_context(tc.tile_pool(name="const", bufs=1))
-        big = ctx.enter_context(tc.tile_pool(name="big", bufs=1))
-        grp = ctx.enter_context(tc.tile_pool(name="grp", bufs=5))
-        codes = ctx.enter_context(tc.tile_pool(name="codes", bufs=3))
+        inputs = ctx.enter_context(tc.tile_pool(name="inputs", bufs=1))
+        regroup = ctx.enter_context(tc.tile_pool(name="regroup", bufs=5))
+        w_mx = ctx.enter_context(tc.tile_pool(name="w_mx", bufs=3))
         work = ctx.enter_context(tc.tile_pool(name="work", bufs=3))
         psum = ctx.enter_context(tc.psum_pool(name="psum", bufs=4))
 
-        x_sb = [big.tile([P, D], BF16, name="x_sb%d" % t) for t in range(NT)]
-        w_sb = [big.tile([P, 2 * D], BF16, name="w_sb%d" % k) for k in range(NU)]
+        x_rows = [inputs.tile([P, WIDTH], BF16, name="x_rows%d" % t) for t in range(TOKEN_TILES)]
+        w_rows = [inputs.tile([P, 2 * WIDTH], BF16, name="w_rows%d" % unit) for unit in range(UNITS)]
 
         def load_x(t):
-            nc.sync.dma_start(out=x_sb[t][:], in_=x[t * P:(t + 1) * P, :])
+            nc.sync.dma_start(out=x_rows[t][:], in_=x[t * P:(t + 1) * P, :])
 
-        def load_w(k):
-            n, e = CHUNKS[k // 2], k % 2
-            rows = w[n * 512:(n + 1) * 512, :].rearrange("(a p e) k -> e p a k", a=2, e=2)
-            nc.sync.dma_start(out=w_sb[k][:].rearrange("p (a k) -> p a k", a=2), in_=rows[e])
+        def load_w(unit):
+            n, parity = CHUNK_ORDER[unit // 2], unit % 2
+            rows = w[n * 2 * CHUNK_PAIRS:(n + 1) * 2 * CHUNK_PAIRS, :].rearrange("(a p o) k -> o p a k", a=2, o=2)
+            nc.sync.dma_start(out=w_rows[unit][:].rearrange("p (a k) -> p a k", a=2), in_=rows[parity])
 
         load_x(0)
         load_w(0)
-        for t in range(1, NT):
+        for t in range(1, TOKEN_TILES):
             load_x(t)
-        for k in range(1, NU):
-            load_w(k)
+        for unit in range(1, UNITS):
+            load_w(unit)
 
         warm = const.tile([P, 2], F32, name="warm")
         nc.vector.memset(warm[:, 0:1], 0.0)
         nc.scalar.activation(out=warm[:, 1:2], in_=warm[:, 0:1], func=ACT.Sin)
-        ident = const.tile([P, P], F32, name="ident")
-        make_identity(nc, ident[:])
-        s_int = const.tile([P, NT], I32, name="s_int")
-        nc.gpsimd.iota(s_int[:], pattern=[[P, NT]], base=0, channel_multiplier=1)
-        sc = const.tile([P, 16], F32, name="sc")
-        nc.vector.tensor_copy(out=sc[:, 0:4], in_=s_int[:])
-        nc.vector.tensor_scalar(out=sc[:, 4:8], in0=sc[:, 0:4], scalar1=-1.0, scalar2=None, op0=ALU.mult)
-        nc.vector.tensor_scalar(out=sc[:, 8:12], in0=sc[:, 0:4], scalar1=1.0 / TWO_PI, scalar2=None, op0=ALU.mult)
-        nc.vector.memset(sc[:, 12:13], 1.0)
-        nc.vector.tensor_scalar(out=sc[:, 13:14], in0=sc[:, 12:13], scalar1=0.5 * math.pi, scalar2=None, op0=ALU.mult)
-        half_pi = sc[:, 13:14]
+        identity = const.tile([P, P], F32, name="identity")
+        make_identity(nc, identity[:])
+        row_int = const.tile([P, TOKEN_TILES], I32, name="row_int")
+        nc.gpsimd.iota(row_int[:], pattern=[[P, TOKEN_TILES]], base=0, channel_multiplier=1)
+        scalars = const.tile([P, 16], F32, name="scalars")
+        nc.vector.tensor_copy(out=scalars[:, 0:4], in_=row_int[:])
+        nc.vector.tensor_scalar(out=scalars[:, 4:8], in0=scalars[:, 0:4], scalar1=-1.0, scalar2=None, op0=ALU.mult)
+        nc.vector.tensor_scalar(out=scalars[:, 8:12], in0=scalars[:, 0:4], scalar1=1.0 / TWO_PI, scalar2=None,
+                                op0=ALU.mult)
+        nc.vector.memset(scalars[:, 12:13], 1.0)
+        nc.vector.tensor_scalar(out=scalars[:, 13:14], in0=scalars[:, 12:13], scalar1=0.5 * math.pi, scalar2=None,
+                                op0=ALU.mult)
+        half_pi = scalars[:, 13:14]
 
-        freq = const.tile([P, HALF], F32, name="freq")
-        nc.vector.memset(freq[:, 0:1], 1.0)
+        def row(t):
+            return scalars[:, t:t + 1]
+
+        def minus_row(t):
+            return scalars[:, 4 + t:5 + t]
+
+        def row_in_turns(t):
+            return scalars[:, 8 + t:9 + t]
+
+        frequency = const.tile([P, PAIRS], F32, name="frequency")
+        nc.vector.memset(frequency[:, 0:1], 1.0)
         size = 1
-        while size < HALF:
-            for m in range(1, 4):
+        while size < PAIRS:
+            for power in range(1, 4):
                 nc.vector.tensor_scalar(
-                    out=freq[:, m * size:(m + 1) * size], in0=freq[:, 0:size],
-                    scalar1=BASE ** (-(m * size) / HALF), scalar2=None, op0=ALU.mult,
+                    out=frequency[:, power * size:(power + 1) * size], in0=frequency[:, 0:size],
+                    scalar1=BASE ** (-(power * size) / PAIRS), scalar2=None, op0=ALU.mult,
                 )
             size *= 4
 
-        frac = [const.tile([P, 2, THR[tp]], F32, name="frac%d" % tp) for tp in range(2)]
-        afr = [const.tile([P, 2, THR[tp]], F32, name="afr%d" % tp) for tp in range(2)]
-        tab = [const.tile([P, NT, 3, 256], F32, name="tab%d" % n) for n in range(4)]
+        reduced_pairs = [first_small_pair(P * (2 * h + 2) - 1) for h in range(2)]
+        fraction = [const.tile([P, 2, reduced_pairs[h]], F32, name="fraction%d" % h) for h in range(2)]
+        fraction_abs = [const.tile([P, 2, reduced_pairs[h]], F32, name="fraction_abs%d" % h) for h in range(2)]
+        table = [const.tile([P, TOKEN_TILES, 3, CHUNK_PAIRS], F32, name="table%d" % n)
+                 for n in range(len(CHUNK_ORDER))]
 
-        def reduce_turns(t):
-            hi = THR[t // 2]
-            turns = work.tile([P, 576], U32, name="turns", bufs=2)
-            nc.scalar.activation(out=turns[:, 0:hi], in_=freq[:, 0:hi], func=ACT.Copy, scale=sc[:, 8 + t:9 + t])
-            nc.vector.scalar_tensor_tensor(out=frac[t // 2][:, t % 2, :], in0=freq[:, 0:hi], scalar=sc[:, 8 + t:9 + t],
-                                           in1=turns[:, 0:hi].bitcast(I32), op0=ALU.mult, op1=ALU.subtract)
+        def reduce_angles(t):
+            pairs = reduced_pairs[t // 2]
+            turns = work.tile([P, reduced_pairs[1]], U32, name="turns", bufs=2)
+            nc.scalar.activation(out=turns[:, 0:pairs], in_=frequency[:, 0:pairs], func=ACT.Copy,
+                                 scale=row_in_turns(t))
+            nc.vector.scalar_tensor_tensor(out=fraction[t // 2][:, t % 2, :], in0=frequency[:, 0:pairs],
+                                           scalar=row_in_turns(t), in1=turns[:, 0:pairs].bitcast(I32),
+                                           op0=ALU.mult, op1=ALU.subtract)
 
-        def tables_half(c, tp):
-            if c >= len(CHUNKS):
-                return
-            n = CHUNKS[c]
-            lo, hi = 256 * n, 256 * (n + 1)
-            mid = min(max(THR[tp], lo), hi)
-            both = slice(2 * tp, 2 * tp + 2)
-            if mid > lo:
-                nc.scalar.activation(out=afr[tp][:, :, lo:mid], in_=frac[tp][:, :, lo:mid], func=ACT.Abs)
-                nc.scalar.activation(out=tab[n][:, both, 2, 0:mid - lo], in_=frac[tp][:, :, lo:mid], func=ACT.Sin,
-                                     scale=TWO_PI)
-                nc.scalar.activation(out=tab[n][:, both, 1, 0:mid - lo], in_=afr[tp][:, :, lo:mid], func=ACT.Sin,
-                                     scale=-TWO_PI, bias=half_pi)
-            if mid < hi:
-                for t in (2 * tp, 2 * tp + 1):
-                    nc.scalar.activation(out=tab[n][:, t, 2, mid - lo:256], in_=freq[:, mid:hi], func=ACT.Sin,
-                                         scale=sc[:, t:t + 1])
-                    nc.scalar.activation(out=tab[n][:, t, 1, mid - lo:256], in_=freq[:, mid:hi], func=ACT.Sin,
-                                         scale=sc[:, 4 + t:5 + t], bias=half_pi)
-            nc.gpsimd.tensor_scalar(out=tab[n][:, both, 0, :], in0=tab[n][:, both, 2, :],
+        def make_table(n, h):
+            low, high = CHUNK_PAIRS * n, CHUNK_PAIRS * (n + 1)
+            middle = min(max(reduced_pairs[h], low), high)
+            both = slice(2 * h, 2 * h + 2)
+            if middle > low:
+                nc.scalar.activation(out=fraction_abs[h][:, :, low:middle], in_=fraction[h][:, :, low:middle],
+                                     func=ACT.Abs)
+                nc.scalar.activation(out=table[n][:, both, 2, 0:middle - low], in_=fraction[h][:, :, low:middle],
+                                     func=ACT.Sin, scale=TWO_PI)
+                nc.scalar.activation(out=table[n][:, both, 1, 0:middle - low], in_=fraction_abs[h][:, :, low:middle],
+                                     func=ACT.Sin, scale=-TWO_PI, bias=half_pi)
+            if middle < high:
+                for t in (2 * h, 2 * h + 1):
+                    nc.scalar.activation(out=table[n][:, t, 2, middle - low:CHUNK_PAIRS],
+                                         in_=frequency[:, middle:high], func=ACT.Sin, scale=row(t))
+                    nc.scalar.activation(out=table[n][:, t, 1, middle - low:CHUNK_PAIRS],
+                                         in_=frequency[:, middle:high], func=ACT.Sin, scale=minus_row(t), bias=half_pi)
+            nc.gpsimd.tensor_scalar(out=table[n][:, both, 0, :], in0=table[n][:, both, 2, :],
                                     scalar1=-1.0, scalar2=0.0, op0=ALU.mult, op1=ALU.add)
 
-        x_codes = [big.tile([P, 512], U32, name="x_codes%d" % t, align_bytes=64) for t in range(NT)]
-        x_scale = [big.tile([P, 512], U8, name="x_scale%d" % t, align_bytes=64) for t in range(NT)]
+        x_codes = [inputs.tile([P, PASSES * P], U32, name="x_codes%d" % t, align_bytes=64) for t in range(TOKEN_TILES)]
+        x_scales = [inputs.tile([P, PASSES * P], U8, name="x_scales%d" % t, align_bytes=64) for t in range(TOKEN_TILES)]
 
-        def x_tile(t):
-            xw = x_sb[t][:].bitcast(F32)
-            g4 = grp.tile([P, 2048], BF16, name="g4", align_bytes=64)
-            g4w = g4[:].bitcast(F32)
+        def quantise_x(t):
+            words = x_rows[t][:].bitcast(F32)
+            regrouped = regroup.tile([P, 4 * BANK], BF16, name="regrouped", align_bytes=64)
+            regrouped_words = regrouped[:].bitcast(F32)
             for b in range(2):
-                bank = psum.tile([P, 512], F32, name="tp")
-                for gl in range(2):
-                    for u in range(2):
-                        c = 2 * (2 * b + gl) + u
-                        nc.tensor.transpose(bank[:, (2 * gl + u) * P:(2 * gl + u + 1) * P],
-                                            xw[:, c * P:(c + 1) * P], ident[:])
-                dst = g4w[:, b * 512:(b + 1) * 512].rearrange("p (g r u) -> p g r u", g=2, u=2)
-                src = bank[:].rearrange("p (g u r) -> p g r u", g=2, u=2)
-                if X_EVAC[b] == "v":
-                    nc.vector.tensor_copy(out=dst, in_=src)
-                else:
-                    nc.scalar.copy(out=dst, in_=src)
-            nc.vector.quantize_mx(out=x_codes[t][:].bitcast(FP8X4), scales=x_scale[t][:], in_=g4[:])
+                flipped = psum.tile([P, BANK], F32, name="flipped")
+                for place in range(4):
+                    block = 4 * b + place
+                    nc.tensor.transpose(flipped[:, place * P:(place + 1) * P], words[:, block * P:(block + 1) * P],
+                                        identity[:])
+                nc.scalar.copy(
+                    out=regrouped_words[:, b * BANK:(b + 1) * BANK].rearrange("p (g r u) -> p g r u", g=2, u=2),
+                    in_=flipped[:].rearrange("p (g u r) -> p g r u", g=2, u=2),
+                )
+            nc.vector.quantize_mx(out=x_codes[t][:].bitcast(FP8X4), scales=x_scales[t][:], in_=regrouped[:])
 
         w_codes = {}
-        w_scale = {}
+        w_scales = {}
 
-        def w_unit(k):
-            ww = w_sb[k][:].bitcast(F32)
-            w_codes[k] = codes.tile([P, 1024], U32, name="w_codes", align_bytes=64)
-            w_scale[k] = codes.tile([P, 1024], U8, name="w_scale", align_bytes=64)
-            for h in range(2):
-                g4 = grp.tile([P, 2048], BF16, name="g4", align_bytes=64)
-                g4w = g4[:].bitcast(F32)
-                for gl in range(2):
-                    g = 2 * h + gl
-                    bank = psum.tile([P, 512], F32, name="tp")
+        def quantise_w(unit):
+            words = w_rows[unit][:].bitcast(F32)
+            w_codes[unit] = w_mx.tile([P, PASSES * CHUNK_PAIRS], U32, name="w_codes", align_bytes=64)
+            w_scales[unit] = w_mx.tile([P, PASSES * CHUNK_PAIRS], U8, name="w_scales", align_bytes=64)
+            for first_pass in range(0, PASSES, 2):
+                regrouped = regroup.tile([P, 4 * BANK], BF16, name="regrouped", align_bytes=64)
+                regrouped_words = regrouped[:].bitcast(F32)
+                for b in range(2):
+                    g = first_pass + b
+                    flipped = psum.tile([P, BANK], F32, name="flipped")
                     for u in range(2):
-                        for e in range(2):
-                            c0 = e * 1024 + (2 * g + u) * P
-                            nc.tensor.transpose(bank[:, (2 * u + e) * P:(2 * u + e + 1) * P],
-                                                ww[:, c0:c0 + P], ident[:])
-                    dst = g4w[:, gl * 512:(gl + 1) * 512].rearrange("p (c u) -> p c u", u=2)
-                    src = bank[:].rearrange("p (u c) -> p c u", u=2)
-                    if k < W_EVAC_V and gl == 1:
-                        nc.vector.tensor_copy(out=dst, in_=src)
+                        for a in range(2):
+                            first_word = a * PAIRS + (2 * g + u) * P
+                            nc.tensor.transpose(flipped[:, (2 * u + a) * P:(2 * u + a + 1) * P],
+                                                words[:, first_word:first_word + P], identity[:])
+                    target = regrouped_words[:, b * BANK:(b + 1) * BANK].rearrange("p (r u) -> p r u", u=2)
+                    source = flipped[:].rearrange("p (u r) -> p r u", u=2)
+                    if unit < SHARED_UNITS and b == 1:
+                        nc.vector.tensor_copy(out=target, in_=source)
                     else:
-                        nc.scalar.copy(out=dst, in_=src)
-                nc.vector.quantize_mx(out=w_codes[k][:, h * 512:(h + 1) * 512].bitcast(FP8X4),
-                                      scales=w_scale[k][:, h * 512:(h + 1) * 512], in_=g4[:])
+                        nc.scalar.copy(out=target, in_=source)
+                columns = slice(first_pass * CHUNK_PAIRS, (first_pass + 2) * CHUNK_PAIRS)
+                nc.vector.quantize_mx(out=w_codes[unit][:, columns].bitcast(FP8X4), scales=w_scales[unit][:, columns],
+                                      in_=regrouped[:])
 
-        first_products = {}
+        even_products = {}
 
-        def mx_unit(k):
-            n, e = CHUNKS[k // 2], k % 2
-            last = k == NU - 1
-            groups = [(t,) for t in range(NT)] if last else [(0, 1), (2, 3)]
-            for tiles in groups:
-                nt = len(tiles)
-                y = psum.tile([P, 512], F32, name="tp" if last else "y")
-                for j, t in enumerate(tiles):
-                    for g in range(NG):
+        def multiply_and_rotate(unit):
+            n, parity = CHUNK_ORDER[unit // 2], unit % 2
+            last = unit == UNITS - 1
+            for tiles in ([(t,) for t in range(TOKEN_TILES)] if last else [(0, 1), (2, 3)]):
+                sums = psum.tile([P, BANK], F32, name="flipped" if last else "sums")
+                for place, t in enumerate(tiles):
+                    for g in range(PASSES):
                         nc.tensor.matmul_mx(
-                            out=y[:, j * 256:(j + 1) * 256],
+                            out=sums[:, place * CHUNK_PAIRS:(place + 1) * CHUNK_PAIRS],
                             lhsT=x_codes[t][:, g * P:(g + 1) * P].bitcast(FP8X4),
-                            lhsT_scale=x_scale[t][:, g * P:(g + 1) * P],
-                            rhs=w_codes[k][:, g * 256:(g + 1) * 256].bitcast(FP8X4),
-                            rhs_scale=w_scale[k][:, g * 256:(g + 1) * 256],
-                            start=(g == 0), stop=(g == NG - 1),
+                            lhsT_scale=x_scales[t][:, g * P:(g + 1) * P],
+                            rhs=w_codes[unit][:, g * CHUNK_PAIRS:(g + 1) * CHUNK_PAIRS].bitcast(FP8X4),
+                            rhs_scale=w_scales[unit][:, g * CHUNK_PAIRS:(g + 1) * CHUNK_PAIRS],
+                            start=(g == 0), stop=(g == PASSES - 1),
                         )
-                prod = work.tile([P, 2, 256, 2], F32, name="pa" if e == 0 else "pb", bufs=4 if e == 0 else 3)
+                products = work.tile([P, 2, CHUNK_PAIRS, 2], F32,
+                                     name="even_products" if parity == 0 else "odd_products",
+                                     bufs=4 if parity == 0 else 3)
                 nc.vector.tensor_tensor(
-                    out=prod[:, 0:nt],
-                    in0=y[:, 0:nt * 256].rearrange("p (t r) -> p t r", t=nt).unsqueeze(3).to_broadcast([P, nt, 256, 2]),
-                    in1=tab[n][:, tiles[0]:tiles[0] + nt, 1 - e:3 - e, :].rearrange("p t c r -> p t r c"),
+                    out=products[:, 0:len(tiles)],
+                    in0=sums[:, 0:len(tiles) * CHUNK_PAIRS].rearrange("p (t r) -> p t r", t=len(tiles)).unsqueeze(3)
+                    .to_broadcast([P, len(tiles), CHUNK_PAIRS, 2]),
+                    in1=table[n][:, tiles[0]:tiles[0] + len(tiles), 1 - parity:3 - parity, :]
+                    .rearrange("p t c r -> p t r c"),
                     op=ALU.mult,
                 )
-                if e == 0:
-                    first_products[tiles[0] // 2] = prod
+                if parity == 0:
+                    even_products[tiles[0] // 2] = products
                 else:
-                    eng = nc.vector if (last and tiles[0] >= LAST_ON_VECTOR) else nc.gpsimd
-                    for j, t in enumerate(tiles):
-                        res = first_products[t // 2][:, t % 2]
-                        eng.tensor_tensor(out=res, in0=res, in1=prod[:, j], op=ALU.add)
-                        nc.sync.dma_start(out=out[t * P:(t + 1) * P, n * 512:(n + 1) * 512],
-                                          in_=res.rearrange("p r c -> p (r c)"))
+                    adder = nc.vector if (last and tiles[0] >= 2) else nc.gpsimd
+                    for place, t in enumerate(tiles):
+                        rotated = even_products[t // 2][:, t % 2]
+                        adder.tensor_tensor(out=rotated, in0=rotated, in1=products[:, place], op=ALU.add)
+                        nc.sync.dma_start(out=out[t * P:(t + 1) * P, n * 2 * CHUNK_PAIRS:(n + 1) * 2 * CHUNK_PAIRS],
+                                          in_=rotated.rearrange("p r c -> p (r c)"))
 
-        for t in range(NT):
-            reduce_turns(t)
-        if HEAD == 0:
-            x_tile(0)
-            w_unit(0)
-            for t in range(1, NT):
-                x_tile(t)
-            tables_half(0, 0)
-            tables_half(0, 1)
-        elif HEAD == 1:
-            tables_half(0, 0)
-            x_tile(0)
-            w_unit(0)
-            tables_half(0, 1)
-            for t in range(1, NT):
-                x_tile(t)
-        mx_unit(0)
-        for k in range(1, NU + 1):
-            if k < NU:
-                w_unit(k)
-                tables_half((k + 1) // 2, (k + 1) % 2)
-            if k > 1:
-                mx_unit(k - 1)
+        for t in range(TOKEN_TILES):
+            reduce_angles(t)
+        quantise_x(0)
+        quantise_w(0)
+        for t in range(1, TOKEN_TILES):
+            quantise_x(t)
+        make_table(CHUNK_ORDER[0], 0)
+        make_table(CHUNK_ORDER[0], 1)
+        multiply_and_rotate(0)
+        for unit in range(1, UNITS):
+            quantise_w(unit)
+            if unit + 1 < UNITS:
+                make_table(CHUNK_ORDER[(unit + 1) // 2], (unit + 1) % 2)
+            if unit > 1:
+                multiply_and_rotate(unit - 1)
+        multiply_and_rotate(UNITS - 1)

import math
from contextlib import ExitStack

import concourse.mybir as mybir
from concourse.masks import make_identity

F32 = mybir.dt.float32
BF16 = mybir.dt.bfloat16
I32 = mybir.dt.int32
U32 = mybir.dt.uint32
U8 = mybir.dt.uint8
FP8X4 = mybir.dt.float8_e4m3fn_x4
ALU = mybir.AluOpType
ACT = mybir.ActivationFunctionType

P = 128
TOKENS, WIDTH = 512, 2048
PAIRS = WIDTH // 2
BASE = 10000.0
FLOPS = 2 * TOKENS * WIDTH * WIDTH

BANK = 512
TOKEN_TILES = TOKENS // P
PASSES = WIDTH // (4 * P)
CHUNK_PAIRS = 256
CHUNK_ORDER = (3, 2, 1, 0)
UNITS = 2 * len(CHUNK_ORDER)
SHARED_UNITS = 2
TWO_PI = 2.0 * math.pi


def first_small_pair(row):
    pair = 0
    while row * BASE ** (-pair / PAIRS) > math.pi:
        pair += 16
    return pair


def tile_ropeattention_pa_kernel(tc, x, w, out):
    nc = tc.nc
    with ExitStack() as ctx:
        const = ctx.enter_context(tc.tile_pool(name="const", bufs=1))
        inputs = ctx.enter_context(tc.tile_pool(name="inputs", bufs=1))
        regroup = ctx.enter_context(tc.tile_pool(name="regroup", bufs=5))
        w_mx = ctx.enter_context(tc.tile_pool(name="w_mx", bufs=3))
        work = ctx.enter_context(tc.tile_pool(name="work", bufs=3))
        psum = ctx.enter_context(tc.psum_pool(name="psum", bufs=4))

        x_rows = [inputs.tile([P, WIDTH], BF16, name="x_rows%d" % t) for t in range(TOKEN_TILES)]
        w_rows = [inputs.tile([P, 2 * WIDTH], BF16, name="w_rows%d" % unit) for unit in range(UNITS)]

        def load_x(t):
            nc.sync.dma_start(out=x_rows[t][:], in_=x[t * P:(t + 1) * P, :])

        def load_w(unit):
            n, parity = CHUNK_ORDER[unit // 2], unit % 2
            rows = w[n * 2 * CHUNK_PAIRS:(n + 1) * 2 * CHUNK_PAIRS, :].rearrange("(a p o) k -> o p a k", a=2, o=2)
            nc.sync.dma_start(out=w_rows[unit][:].rearrange("p (a k) -> p a k", a=2), in_=rows[parity])

        load_x(0)
        load_w(0)
        for t in range(1, TOKEN_TILES):
            load_x(t)
        for unit in range(1, UNITS):
            load_w(unit)

        warm = const.tile([P, 2], F32, name="warm")
        nc.vector.memset(warm[:, 0:1], 0.0)
        nc.scalar.activation(out=warm[:, 1:2], in_=warm[:, 0:1], func=ACT.Sin)
        identity = const.tile([P, P], F32, name="identity")
        make_identity(nc, identity[:])
        row_int = const.tile([P, TOKEN_TILES], I32, name="row_int")
        nc.gpsimd.iota(row_int[:], pattern=[[P, TOKEN_TILES]], base=0, channel_multiplier=1)
        scalars = const.tile([P, 16], F32, name="scalars")
        nc.vector.tensor_copy(out=scalars[:, 0:4], in_=row_int[:])
        nc.vector.tensor_scalar(out=scalars[:, 4:8], in0=scalars[:, 0:4], scalar1=-1.0, scalar2=None, op0=ALU.mult)
        nc.vector.tensor_scalar(out=scalars[:, 8:12], in0=scalars[:, 0:4], scalar1=1.0 / TWO_PI, scalar2=None,
                                op0=ALU.mult)
        nc.vector.memset(scalars[:, 12:13], 1.0)
        nc.vector.tensor_scalar(out=scalars[:, 13:14], in0=scalars[:, 12:13], scalar1=0.5 * math.pi, scalar2=None,
                                op0=ALU.mult)
        half_pi = scalars[:, 13:14]

        def row(t):
            return scalars[:, t:t + 1]

        def minus_row(t):
            return scalars[:, 4 + t:5 + t]

        def row_in_turns(t):
            return scalars[:, 8 + t:9 + t]

        frequency = const.tile([P, PAIRS], F32, name="frequency")
        nc.vector.memset(frequency[:, 0:1], 1.0)
        size = 1
        while size < PAIRS:
            for power in range(1, 4):
                nc.vector.tensor_scalar(
                    out=frequency[:, power * size:(power + 1) * size], in0=frequency[:, 0:size],
                    scalar1=BASE ** (-(power * size) / PAIRS), scalar2=None, op0=ALU.mult,
                )
            size *= 4

        reduced_pairs = [first_small_pair(P * (2 * h + 2) - 1) for h in range(2)]
        fraction = [const.tile([P, 2, reduced_pairs[h]], F32, name="fraction%d" % h) for h in range(2)]
        fraction_abs = [const.tile([P, 2, reduced_pairs[h]], F32, name="fraction_abs%d" % h) for h in range(2)]
        table = [const.tile([P, TOKEN_TILES, 3, CHUNK_PAIRS], F32, name="table%d" % n)
                 for n in range(len(CHUNK_ORDER))]

        def reduce_angles(t):
            pairs = reduced_pairs[t // 2]
            turns = work.tile([P, reduced_pairs[1]], U32, name="turns", bufs=2)
            nc.scalar.activation(out=turns[:, 0:pairs], in_=frequency[:, 0:pairs], func=ACT.Copy,
                                 scale=row_in_turns(t))
            nc.vector.scalar_tensor_tensor(out=fraction[t // 2][:, t % 2, :], in0=frequency[:, 0:pairs],
                                           scalar=row_in_turns(t), in1=turns[:, 0:pairs].bitcast(I32),
                                           op0=ALU.mult, op1=ALU.subtract)

        def make_table(n, h):
            low, high = CHUNK_PAIRS * n, CHUNK_PAIRS * (n + 1)
            middle = min(max(reduced_pairs[h], low), high)
            both = slice(2 * h, 2 * h + 2)
            if middle > low:
                nc.scalar.activation(out=fraction_abs[h][:, :, low:middle], in_=fraction[h][:, :, low:middle],
                                     func=ACT.Abs)
                nc.scalar.activation(out=table[n][:, both, 2, 0:middle - low], in_=fraction[h][:, :, low:middle],
                                     func=ACT.Sin, scale=TWO_PI)
                nc.scalar.activation(out=table[n][:, both, 1, 0:middle - low], in_=fraction_abs[h][:, :, low:middle],
                                     func=ACT.Sin, scale=-TWO_PI, bias=half_pi)
            if middle < high:
                for t in (2 * h, 2 * h + 1):
                    nc.scalar.activation(out=table[n][:, t, 2, middle - low:CHUNK_PAIRS],
                                         in_=frequency[:, middle:high], func=ACT.Sin, scale=row(t))
                    nc.scalar.activation(out=table[n][:, t, 1, middle - low:CHUNK_PAIRS],
                                         in_=frequency[:, middle:high], func=ACT.Sin, scale=minus_row(t), bias=half_pi)
            nc.gpsimd.tensor_scalar(out=table[n][:, both, 0, :], in0=table[n][:, both, 2, :],
                                    scalar1=-1.0, scalar2=0.0, op0=ALU.mult, op1=ALU.add)

        x_codes = [inputs.tile([P, PASSES * P], U32, name="x_codes%d" % t, align_bytes=64) for t in range(TOKEN_TILES)]
        x_scales = [inputs.tile([P, PASSES * P], U8, name="x_scales%d" % t, align_bytes=64) for t in range(TOKEN_TILES)]

        def quantise_x(t):
            words = x_rows[t][:].bitcast(F32)
            regrouped = regroup.tile([P, 4 * BANK], BF16, name="regrouped", align_bytes=64)
            regrouped_words = regrouped[:].bitcast(F32)
            for b in range(2):
                flipped = psum.tile([P, BANK], F32, name="flipped")
                for place in range(4):
                    block = 4 * b + place
                    nc.tensor.transpose(flipped[:, place * P:(place + 1) * P], words[:, block * P:(block + 1) * P],
                                        identity[:])
                nc.scalar.copy(
                    out=regrouped_words[:, b * BANK:(b + 1) * BANK].rearrange("p (g r u) -> p g r u", g=2, u=2),
                    in_=flipped[:].rearrange("p (g u r) -> p g r u", g=2, u=2),
                )
            nc.vector.quantize_mx(out=x_codes[t][:].bitcast(FP8X4), scales=x_scales[t][:], in_=regrouped[:])

        w_codes = {}
        w_scales = {}

        def quantise_w(unit):
            words = w_rows[unit][:].bitcast(F32)
            w_codes[unit] = w_mx.tile([P, PASSES * CHUNK_PAIRS], U32, name="w_codes", align_bytes=64)
            w_scales[unit] = w_mx.tile([P, PASSES * CHUNK_PAIRS], U8, name="w_scales", align_bytes=64)
            for first_pass in range(0, PASSES, 2):
                regrouped = regroup.tile([P, 4 * BANK], BF16, name="regrouped", align_bytes=64)
                regrouped_words = regrouped[:].bitcast(F32)
                for b in range(2):
                    g = first_pass + b
                    flipped = psum.tile([P, BANK], F32, name="flipped")
                    for u in range(2):
                        for a in range(2):
                            first_word = a * PAIRS + (2 * g + u) * P
                            nc.tensor.transpose(flipped[:, (2 * u + a) * P:(2 * u + a + 1) * P],
                                                words[:, first_word:first_word + P], identity[:])
                    target = regrouped_words[:, b * BANK:(b + 1) * BANK].rearrange("p (r u) -> p r u", u=2)
                    source = flipped[:].rearrange("p (u r) -> p r u", u=2)
                    if unit < SHARED_UNITS and b == 1:
                        nc.vector.tensor_copy(out=target, in_=source)
                    else:
                        nc.scalar.copy(out=target, in_=source)
                columns = slice(first_pass * CHUNK_PAIRS, (first_pass + 2) * CHUNK_PAIRS)
                nc.vector.quantize_mx(out=w_codes[unit][:, columns].bitcast(FP8X4), scales=w_scales[unit][:, columns],
                                      in_=regrouped[:])

        even_products = {}

        def multiply_and_rotate(unit):
            n, parity = CHUNK_ORDER[unit // 2], unit % 2
            last = unit == UNITS - 1
            for tiles in ([(t,) for t in range(TOKEN_TILES)] if last else [(0, 1), (2, 3)]):
                sums = psum.tile([P, BANK], F32, name="flipped" if last else "sums")
                for place, t in enumerate(tiles):
                    for g in range(PASSES):
                        nc.tensor.matmul_mx(
                            out=sums[:, place * CHUNK_PAIRS:(place + 1) * CHUNK_PAIRS],
                            lhsT=x_codes[t][:, g * P:(g + 1) * P].bitcast(FP8X4),
                            lhsT_scale=x_scales[t][:, g * P:(g + 1) * P],
                            rhs=w_codes[unit][:, g * CHUNK_PAIRS:(g + 1) * CHUNK_PAIRS].bitcast(FP8X4),
                            rhs_scale=w_scales[unit][:, g * CHUNK_PAIRS:(g + 1) * CHUNK_PAIRS],
                            start=(g == 0), stop=(g == PASSES - 1),
                        )
                products = work.tile([P, 2, CHUNK_PAIRS, 2], F32,
                                     name="even_products" if parity == 0 else "odd_products",
                                     bufs=4 if parity == 0 else 3)
                nc.vector.tensor_tensor(
                    out=products[:, 0:len(tiles)],
                    in0=sums[:, 0:len(tiles) * CHUNK_PAIRS].rearrange("p (t r) -> p t r", t=len(tiles)).unsqueeze(3)
                    .to_broadcast([P, len(tiles), CHUNK_PAIRS, 2]),
                    in1=table[n][:, tiles[0]:tiles[0] + len(tiles), 1 - parity:3 - parity, :]
                    .rearrange("p t c r -> p t r c"),
                    op=ALU.mult,
                )
                if parity == 0:
                    even_products[tiles[0] // 2] = products
                else:
                    adder = nc.vector if (last and tiles[0] >= 2) else nc.gpsimd
                    for place, t in enumerate(tiles):
                        rotated = even_products[t // 2][:, t % 2]
                        adder.tensor_tensor(out=rotated, in0=rotated, in1=products[:, place], op=ALU.add)
                        nc.sync.dma_start(out=out[t * P:(t + 1) * P, n * 2 * CHUNK_PAIRS:(n + 1) * 2 * CHUNK_PAIRS],
                                          in_=rotated.rearrange("p r c -> p (r c)"))

        for t in range(TOKEN_TILES):
            reduce_angles(t)
        quantise_x(0)
        quantise_w(0)
        for t in range(1, TOKEN_TILES):
            quantise_x(t)
        make_table(CHUNK_ORDER[0], 0)
        make_table(CHUNK_ORDER[0], 1)
        multiply_and_rotate(0)
        for unit in range(1, UNITS):
            quantise_w(unit)
            if unit + 1 < UNITS:
                make_table(CHUNK_ORDER[(unit + 1) // 2], (unit + 1) % 2)
            if unit > 1:
                multiply_and_rotate(unit - 1)
        multiply_and_rotate(UNITS - 1)
